import numpy as np
import ml_dtypes


def mxq(x, axis, fmt="e4m3"):
    dtype, down = {"e4m3": (ml_dtypes.float8_e4m3fn, 7), "e5m2": (ml_dtypes.float8_e5m2, 14)}[fmt]
    v = np.moveaxis(np.asarray(x, np.float32).astype(ml_dtypes.bfloat16).astype(np.float64), axis, -1)
    blocks = v.reshape(v.shape[:-1] + (-1, 32))
    amax = np.abs(blocks).max(-1, keepdims=True)
    byte = np.maximum(np.where(amax > 0, np.frexp(amax)[1] - 1 + 127, 0) - down, 1)
    scale = np.exp2(byte - 127.0)
    codes = (blocks / scale).astype(np.float32).astype(dtype).astype(np.float64)
    return np.moveaxis((codes * scale).reshape(v.shape), -1, axis)


WIDE = False


def mx_kscale(k):
    if not WIDE:
        return np.ones(k)
    levels = np.array([10, -10, 5, -5, 0])
    a = np.random.permutation(np.resize(levels, k // 512 * 4)).reshape(k // 512, 4)
    idx = np.arange(k)
    return np.exp2(a[idx // 512, idx % 128 // 32])


BF16 = ml_dtypes.bfloat16


def bf(x):
    return np.asarray(x, np.float32).astype(BF16)


def f64(x):
    return np.asarray(x).astype(np.float64)


B, IN_DIM, MEM = 2048, 3840, 256
DIN = MEM + IN_DIM
MIN_TS, MAX_TS, EPS = 0.1, 10.0, 1e-6


def sigmoid(v):
    return 1.0 / (1.0 + np.exp(-v))


def setup_inputs():
    s = mx_kscale(DIN)[MEM:]
    r = np.concatenate([np.ones(MEM), s])
    return {"x": bf(np.random.standard_normal((B, IN_DIM)) * s),
            "h": bf(np.random.standard_normal((B, MEM))),
            "h_candidate": bf(np.tanh(0.7 * np.random.standard_normal((B, MEM)))),
            "Wd": bf(np.random.standard_normal((DIN, MEM)) * 1.3 / np.sqrt(DIN) / r[:, None]),
            "bd": bf(np.random.standard_normal(MEM) * 0.5),
            "Wu": bf(np.random.standard_normal((DIN, MEM)) * 1.3 / np.sqrt(DIN) / r[:, None]),
            "bu": bf(np.random.standard_normal(MEM) * 0.5)}


def reference(x, h, h_candidate, Wd, bd, Wu, bu):
    h = f64(h)
    cq = mxq(np.concatenate([h, f64(x)], axis=-1), 1, "e4m3")
    decay = sigmoid((cq @ mxq(f64(Wd), 0, "e4m3")) + f64(bd))
    update = sigmoid((cq @ mxq(f64(Wu), 0, "e4m3")) + f64(bu))
    decay = MIN_TS + (MAX_TS - MIN_TS) * decay + EPS
    new_h = (1.0 - update) * (h / decay) + update * f64(h_candidate)
    h_norm = np.maximum(np.sqrt(np.square(h).sum(-1, keepdims=True)), EPS)
    nh_norm = np.maximum(np.sqrt(np.square(new_h).sum(-1, keepdims=True)), 1e-12)
    return new_h / nh_norm * h_norm

@@ -1,0 +1,287 @@
+from contextlib import ExitStack
+import math
+
+import concourse.mybir as mybir
+from concourse.masks import make_identity
+
+F32 = mybir.dt.float32
+BF16 = mybir.dt.bfloat16
+U32 = mybir.dt.uint32
+U8 = mybir.dt.uint8
+FP8X4 = mybir.dt.float8_e4m3fn_x4
+ALU = mybir.AluOpType
+ACT = mybir.ActivationFunctionType
+
+P = 128
+B, IN_DIM, MEM = 2048, 3840, 256
+DIN = MEM + IN_DIM
+NT = B // P
+NG = DIN // 512
+NOUT = 2 * MEM
+FLOPS = 2 * B * DIN * NOUT
+
+A0 = 0.1 + 1e-6
+B0 = 10.0 - 0.1
+LNK = math.log((A0 + B0) / A0)
+BETA = B0 / (A0 * (A0 + B0))
+C2 = A0 / B0
+
+MANUAL = False
+XB = 8
+NP1 = 4
+E2_LIST = {4: [0], 5: [1], 6: [2, 3], 7: [4], 8: [5], 9: [6], 10: [7, 8], 11: [9],
+           12: [10], 13: [11], 14: [12, 13], 15: [14]}
+
+H_STEPS = {5: 1, 8: 2, 11: 3}
+
+
+def tile_liquidmemorycell_pb_kernel(tc, x, h, h_candidate, Wd, bd, Wu, bu, out):
+    nc = tc.nc
+    with ExitStack() as ctx:
+        const = ctx.enter_context(tc.tile_pool(name="const", bufs=1))
+        xpool = ctx.enter_context(tc.tile_pool(name="xpool", bufs=XB))
+        work = ctx.enter_context(tc.tile_pool(name="work", bufs=2))
+        psum = ctx.enter_context(tc.psum_pool(name="psum", bufs=4))
+        if MANUAL:
+            ctx.enter_context(tc.manual_schedule())
+
+        xv = x.rearrange("(p t) k -> p t k", t=NT)
+        ov = out.rearrange("(p t) f -> p t f", t=NT)
+        hv = h.rearrange("(p t) f -> p t f", t=NT)
+
+        ident = const.tile([P, P], F32, name="ident")
+        make_identity(nc, ident[:])
+        ones = const.tile([P, P], BF16, name="ones")
+        nc.vector.memset(ones[:], 1.0)
+        brow = const.tile([P, NOUT], BF16, name="brow")
+        nc.vector.memset(brow[:], 0.0)
+        nc.scalar.dma_start(out=brow[0:1, 0:MEM], in_=bd.unsqueeze(0))
+        nc.scalar.dma_start(out=brow[0:1, MEM:NOUT], in_=bu.unsqueeze(0))
+        warm = const.tile([P, 1], F32, name="warm")
+        nc.vector.memset(warm[:], 0.0)
+        warm2 = const.tile([P, 1], F32, name="warm2")
+        nc.scalar.activation(out=warm2[:], in_=warm[:], func=ACT.Sigmoid)
+        neghalf = const.tile([P, 1], F32, name="neghalf")
+        nc.gpsimd.memset(neghalf[:], -0.5)
+        poshalf = const.tile([P, NT], F32, name="poshalf")
+        nc.gpsimd.memset(poshalf[:], 0.5)
+
+        h_all = const.tile([P, NT * MEM], BF16, name="h_all")
+        hc_all = const.tile([P, NT * MEM], BF16, name="hc_all")
+        wr = [const.tile([P, NG, 4, MEM], BF16, name="wr%d" % mi) for mi in range(2)]
+        wcodes = const.tile([P, NG * NOUT], U32, name="wcodes", align_bytes=64)
+        wscl = const.tile([P, NG * NOUT], U8, name="wscl", align_bytes=64)
+        bias = const.tile([P, NOUT], F32, name="bias")
+        hsq = const.tile([P, NT], F32, name="hsq")
+        hmx = const.tile([P, NT], F32, name="hmx")
+        hn = const.tile([P, NT], F32, name="hn")
+        junkh = const.tile([P, MEM], BF16, name="junkh")
+        junkm = const.tile([P, MEM], BF16, name="junkm")
+
+        xs = {}
+        grp = {}
+        codes = {}
+        scl = {}
+        acc = {}
+        gts = {}
+        ms = {}
+        rms = {}
+
+        def load_x(i):
+            xt = xpool.tile([P, DIN], BF16, name="xt", tag="xt")
+            head = xt[:, 0:512].rearrange("p (a w f) -> p a w f", a=2, w=2)
+            nc.sync.dma_start(out=head[:, :, 0, :], in_=hv[:, i, :].rearrange("p (a f) -> p a f", a=2))
+            nc.sync.dma_start(out=head[:, :, 1, :], in_=xv[:, i, 0:MEM].rearrange("p (a f) -> p a f", a=2))
+            nc.sync.dma_start(out=xt[:, 512:DIN], in_=xv[:, i, MEM:IN_DIM])
+            xs[i] = xt
+
+        def load_w(g):
+            for mi, w in enumerate((Wd, Wu)):
+                if g == 0:
+                    for hf in range(2):
+                        nc.sync.dma_start(
+                            out=wr[mi][64 * hf:64 * (hf + 1), 0].rearrange("p (u e) n -> p u e n", u=2),
+                            in_=w[MEM * hf:MEM * (hf + 1), :].rearrange("(u p e) n -> p u e n", u=2, e=2),
+                        )
+                else:
+                    nc.sync.dma_start(
+                        out=wr[mi][:, g].rearrange("p (u e) n -> p u e n", u=2),
+                        in_=w[512 * g:512 * (g + 1), :].rearrange("(u p e) n -> p u e n", u=2, e=2),
+                    )
+
+        def t_bank(i, b, on_vector=False):
+            if b == 0:
+                grp[i] = work.tile([P, DIN], BF16, name="grp", tag="grp", bufs=3, align_bytes=64)
+            xw = xs[i][:].bitcast(F32)
+            tp = psum.tile([P, 512], F32, name="tp", tag="tp")
+            for s in range(4):
+                j = 4 * b + s
+                nc.tensor.transpose(tp[:, P * s:P * (s + 1)], xw[:, P * j:P * (j + 1)], ident[:])
+            dst = grp[i][:].bitcast(F32)[:, 512 * b:512 * (b + 1)].rearrange(
+                "p (g r u) -> p g r u", g=2, u=2)
+            srcv = tp[:].rearrange("p (g u r) -> p g r u", g=2, u=2)
+            if on_vector:
+                nc.vector.tensor_copy(out=dst, in_=srcv)
+            else:
+                nc.scalar.copy(out=dst, in_=srcv)
+
+        def quant(i):
+            codes[i] = work.tile([P, NG * P], U32, name="codes", tag="codes", bufs=4, align_bytes=64)
+            scl[i] = work.tile([P, NG * P], U8, name="scl", tag="scl", bufs=4, align_bytes=64)
+            for hf in range(2):
+                nc.vector.quantize_mx(
+                    out=codes[i][:, 512 * hf:512 * (hf + 1)].bitcast(FP8X4),
+                    scales=scl[i][:, 512 * hf:512 * (hf + 1)],
+                    in_=grp[i][:, 2048 * hf:2048 * (hf + 1)],
+                )
+
+        wgs = {}
+
+        def w_copy(g):
+            wg = work.tile([P, NOUT, 4], BF16, name="wg", tag="wg", bufs=3, align_bytes=64)
+            wgs[g] = wg
+            for mi in range(2):
+                dst = wg[:, MEM * mi:MEM * (mi + 1), :].rearrange("p (c i) t -> p c t i", i=4)
+                src = wr[mi][:, g].rearrange("p t (c i) -> p c t i", i=4)
+                if mi == 0:
+                    nc.vector.tensor_copy(out=dst, in_=src)
+                else:
+                    nc.scalar.copy(out=dst, in_=src)
+
+        def w_quant(g):
+            nc.vector.quantize_mx(
+                out=wcodes[:, NOUT * g:NOUT * (g + 1)].bitcast(FP8X4),
+                scales=wscl[:, NOUT * g:NOUT * (g + 1)],
+                in_=wgs[g][:].rearrange("p n t -> p (n t)"),
+            )
+
+        def mx(i, g):
+            if g == 0:
+                acc[i] = psum.tile([P, NOUT], F32, name="acc", tag="acc")
+            nc.tensor.matmul_mx(
+                out=acc[i][:],
+                lhsT=codes[i][:, P * g:P * (g + 1)].bitcast(FP8X4),
+                lhsT_scale=scl[i][:, P * g:P * (g + 1)],
+                rhs=wcodes[:, NOUT * g:NOUT * (g + 1)].bitcast(FP8X4),
+                rhs_scale=wscl[:, NOUT * g:NOUT * (g + 1)],
+                start=(g == 0),
+                stop=(g == NG - 1),
+            )
+
+        def h_square(i):
+            nc.scalar.activation(out=junkh[:], in_=h_all[:, MEM * i:MEM * (i + 1)], func=ACT.Square,
+                                 accum_out=hsq[:, i:i + 1])
+
+        def h_norms(q):
+            cols = slice(4 * q, 4 * q + 4)
+            for i in range(4 * q, 4 * q + 4):
+                h_square(i)
+            nc.gpsimd.tensor_scalar_max(out=hmx[:, cols], in0=hsq[:, cols], scalar1=1e-12)
+            nc.gpsimd.tensor_tensor(out=hn[:, cols], in0=hmx[:, cols], in1=poshalf[:, cols], op=ALU.pow)
+
+        def e1(i):
+            s = work.tile([P, NOUT], F32, name="s", tag="s", bufs=2)
+            nc.vector.tensor_tensor(out=s[:], in0=acc[i][:], in1=bias[:], op=ALU.add)
+            gt = work.tile([P, NOUT], F32, name="gt", tag="gt", bufs=6)
+            nc.scalar.activation(out=gt[:], in_=s[:], func=ACT.Sigmoid, scale=-1.0)
+            gts[i] = gt
+
+        def e2(i):
+            hs = h_all[:, MEM * i:MEM * (i + 1)]
+            cs = hc_all[:, MEM * i:MEM * (i + 1)]
+            gt = gts[i]
+            w1 = work.tile([P, MEM], F32, name="w1", tag="w1", bufs=2)
+            nc.vector.scalar_tensor_tensor(out=w1[:], in0=gt[:, 0:MEM], scalar=C2, in1=hs,
+                                           op0=ALU.add, op1=ALU.mult)
+            w2 = work.tile([P, MEM], F32, name="w2", tag="w2", bufs=2)
+            nc.vector.scalar_tensor_tensor(out=w2[:], in0=w1[:], scalar=BETA, in1=cs,
+                                           op0=ALU.mult, op1=ALU.subtract)
+            w3 = work.tile([P, MEM], F32, name="w3", tag="w3", bufs=2)
+            nc.vector.tensor_tensor(out=w3[:], in0=w2[:], in1=gt[:, MEM:NOUT], op=ALU.mult)
+            m = work.tile([P, MEM], F32, name="m", tag="m", bufs=4)
+            nc.vector.tensor_tensor(out=m[:], in0=w3[:], in1=cs, op=ALU.add)
+            ms[i] = m
+            sm = work.tile([P, 1], F32, name="sm", tag="sm", bufs=4)
+            nc.scalar.activation(out=junkm[:], in_=m[:], func=ACT.Square, accum_out=sm[:])
+            sx = work.tile([P, 1], F32, name="sx", tag="sx", bufs=4)
+            nc.gpsimd.tensor_scalar_max(out=sx[:], in0=sm[:], scalar1=1e-24)
+            rm = work.tile([P, 1], F32, name="rm", tag="rm", bufs=4)
+            nc.gpsimd.tensor_tensor(out=rm[:], in0=sx[:], in1=neghalf[:], op=ALU.pow)
+            rms[i] = rm
+
+        def e3(i):
+            o = work.tile([P, MEM], F32, name="o", tag="o", bufs=3)
+            nc.vector.tensor_scalar(out=o[:], in0=ms[i][:], scalar1=rms[i][:, 0:1],
+                                    scalar2=hn[:, i:i + 1], op0=ALU.mult, op1=ALU.mult)
+            nc.sync.dma_start(out=ov[:, i, :], in_=o[:])
+
+        load_x(0)
+        for n in range(NP1):
+            if n > 0:
+                load_x(n)
+            load_w(2 * n)
+            load_w(2 * n + 1)
+        load_x(4)
+        nc.sync.dma_start(out=h_all[:], in_=h.rearrange("(p t) f -> p (t f)", t=NT))
+        nc.sync.dma_start(out=hc_all[:], in_=h_candidate.rearrange("(p t) f -> p (t f)", t=NT))
+        for i in range(5, XB):
+            load_x(i)
+
+        bias_ps = psum.tile([P, NOUT], F32, name="bias_ps", tag="acc")
+        nc.tensor.matmul(out=bias_ps[:], lhsT=ones[:], rhs=brow[:], start=True, stop=True)
+        nc.vector.tensor_scalar_add(out=bias[:, 0:MEM], in0=bias_ps[:, 0:MEM], scalar1=LNK)
+        nc.vector.tensor_copy(out=bias[:, MEM:NOUT], in_=bias_ps[:, MEM:NOUT])
+
+        for n in range(NP1):
+            for b in range(4):
+                t_bank(n, b, on_vector=(b == 3))
+            load_x(n + XB)
+            quant(n)
+            w_copy(2 * n)
+            w_copy(2 * n + 1)
+            w_quant(2 * n)
+            w_quant(2 * n + 1)
+            for g in range(2 * n):
+                mx(n, g)
+            for g in (2 * n, 2 * n + 1):
+                for i in range(n + 1):
+                    mx(i, g)
+        h_norms(0)
+
+        t_bank(4, 0)
+        e1(0)
+        t_bank(4, 1)
+        e1(1)
+        t_bank(4, 2)
+        t_bank(4, 3)
+        load_x(4 + XB)
+        quant(4)
+        t_bank(5, 0)
+        e1(2)
+        t_bank(5, 1)
+        e1(3)
+        t_bank(5, 2)
+        t_bank(5, 3)
+        load_x(5 + XB)
+
+        for k in range(NP1, NT):
+            for i in E2_LIST[k]:
+                e2(i)
+            if k + 1 < NT:
+                quant(k + 1)
+            for g in range(NG):
+                mx(k, g)
+            for i in E2_LIST[k]:
+                e3(i)
+            if k in H_STEPS:
+                h_norms(H_STEPS[k])
+            if k + 2 < NT:
+                t_bank(k + 2, 0)
+            e1(k)
+            if k + 2 < NT:
+                for b in range(1, 4):
+                    t_bank(k + 2, b)
+                if k + 2 + XB < NT:
+                    load_x(k + 2 + XB)
+        e2(NT - 1)
+        e3(NT - 1)

@@ -26,7 +26,7 @@ LNK = math.log((A0 + B0) / A0)
 BETA = B0 / (A0 * (A0 + B0))
 C2 = A0 / B0
 
-MANUAL = False
+MANUAL = True
 XB = 8
 NP1 = 4
 E2_LIST = {4: [0], 5: [1], 6: [2, 3], 7: [4], 8: [5], 9: [6], 10: [7, 8], 11: [9],
@@ -221,10 +221,16 @@ def tile_liquidmemorycell_pb_kernel(tc, x, h, h_candidate, Wd, bd, Wu, bu, out):
                 load_x(n)
             load_w(2 * n)
             load_w(2 * n + 1)
+        hflat = h.rearrange("(p t) f -> p (t f)", t=NT)
+        cflat = h_candidate.rearrange("(p t) f -> p (t f)", t=NT)
+        cut = NP1 * MEM
+        nc.sync.dma_start(out=h_all[:, 0:cut], in_=hflat[:, 0:cut])
+        nc.sync.dma_start(out=hc_all[:, 0:cut], in_=cflat[:, 0:cut])
         load_x(4)
-        nc.sync.dma_start(out=h_all[:], in_=h.rearrange("(p t) f -> p (t f)", t=NT))
-        nc.sync.dma_start(out=hc_all[:], in_=h_candidate.rearrange("(p t) f -> p (t f)", t=NT))
-        for i in range(5, XB):
+        load_x(5)
+        nc.sync.dma_start(out=h_all[:, cut:NT * MEM], in_=hflat[:, cut:NT * MEM])
+        nc.sync.dma_start(out=hc_all[:, cut:NT * MEM], in_=cflat[:, cut:NT * MEM])
+        for i in range(6, XB):
             load_x(i)
 
         bias_ps = psum.tile([P, NOUT], F32, name="bias_ps", tag="acc")
@@ -246,7 +252,6 @@ def tile_liquidmemorycell_pb_kernel(tc, x, h, h_candidate, Wd, bd, Wu, bu, out):
             for g in (2 * n, 2 * n + 1):
                 for i in range(n + 1):
                     mx(i, g)
-        h_norms(0)
 
         t_bank(4, 0)
         e1(0)
@@ -263,6 +268,7 @@ def tile_liquidmemorycell_pb_kernel(tc, x, h, h_candidate, Wd, bd, Wu, bu, out):
         t_bank(5, 2)
         t_bank(5, 3)
         load_x(5 + XB)
+        h_norms(0)
 
         for k in range(NP1, NT):
             for i in E2_LIST[k]:

@@ -29,10 +29,8 @@ C2 = A0 / B0
 MANUAL = True
 XB = 8
 NP1 = 4
-E2_LIST = {4: [0], 5: [1], 6: [2, 3], 7: [4], 8: [5], 9: [6], 10: [7, 8], 11: [9],
-           12: [10], 13: [11], 14: [12, 13], 15: [14]}
 
-H_STEPS = {5: 1, 8: 2, 11: 3}
+H_STEPS = {4: 0, 8: 1, 10: 2, 12: 3}
 
 
 def tile_liquidmemorycell_pb_kernel(tc, x, h, h_candidate, Wd, bd, Wu, bu, out):
@@ -84,6 +82,7 @@ def tile_liquidmemorycell_pb_kernel(tc, x, h, h_candidate, Wd, bd, Wu, bu, out):
         scl = {}
         acc = {}
         gts = {}
+        ss = {}
         ms = {}
         rms = {}
 
@@ -179,14 +178,17 @@ def tile_liquidmemorycell_pb_kernel(tc, x, h, h_candidate, Wd, bd, Wu, bu, out):
             nc.gpsimd.tensor_scalar_max(out=hmx[:, cols], in0=hsq[:, cols], scalar1=1e-12)
             nc.gpsimd.tensor_tensor(out=hn[:, cols], in0=hmx[:, cols], in1=poshalf[:, cols], op=ALU.pow)
 
-        def e1(i):
+        def e1v(i):
             s = work.tile([P, NOUT], F32, name="s", tag="s", bufs=2)
             nc.vector.tensor_tensor(out=s[:], in0=acc[i][:], in1=bias[:], op=ALU.add)
-            gt = work.tile([P, NOUT], F32, name="gt", tag="gt", bufs=6)
-            nc.scalar.activation(out=gt[:], in_=s[:], func=ACT.Sigmoid, scale=-1.0)
+            ss[i] = s
+
+        def e1s(i):
+            gt = work.tile([P, NOUT], F32, name="gt", tag="gt", bufs=3)
+            nc.scalar.activation(out=gt[:], in_=ss[i][:], func=ACT.Sigmoid, scale=-1.0)
             gts[i] = gt
 
-        def e2(i):
+        def e2v(i):
             hs = h_all[:, MEM * i:MEM * (i + 1)]
             cs = hc_all[:, MEM * i:MEM * (i + 1)]
             gt = gts[i]
@@ -201,6 +203,9 @@ def tile_liquidmemorycell_pb_kernel(tc, x, h, h_candidate, Wd, bd, Wu, bu, out):
             m = work.tile([P, MEM], F32, name="m", tag="m", bufs=4)
             nc.vector.tensor_tensor(out=m[:], in0=w3[:], in1=cs, op=ALU.add)
             ms[i] = m
+
+        def e2s(i):
+            m = ms[i]
             sm = work.tile([P, 1], F32, name="sm", tag="sm", bufs=4)
             nc.scalar.activation(out=junkm[:], in_=m[:], func=ACT.Square, accum_out=sm[:])
             sx = work.tile([P, 1], F32, name="sx", tag="sx", bufs=4)
@@ -226,12 +231,10 @@ def tile_liquidmemorycell_pb_kernel(tc, x, h, h_candidate, Wd, bd, Wu, bu, out):
         cut = NP1 * MEM
         nc.sync.dma_start(out=h_all[:, 0:cut], in_=hflat[:, 0:cut])
         nc.sync.dma_start(out=hc_all[:, 0:cut], in_=cflat[:, 0:cut])
-        load_x(4)
-        load_x(5)
+        for i in range(NP1, XB):
+            load_x(i)
         nc.sync.dma_start(out=h_all[:, cut:NT * MEM], in_=hflat[:, cut:NT * MEM])
         nc.sync.dma_start(out=hc_all[:, cut:NT * MEM], in_=cflat[:, cut:NT * MEM])
-        for i in range(6, XB):
-            load_x(i)
 
         bias_ps = psum.tile([P, NOUT], F32, name="bias_ps", tag="acc")
         nc.tensor.matmul(out=bias_ps[:], lhsT=ones[:], rhs=brow[:], start=True, stop=True)
@@ -253,41 +256,28 @@ def tile_liquidmemorycell_pb_kernel(tc, x, h, h_candidate, Wd, bd, Wu, bu, out):
                 for i in range(n + 1):
                     mx(i, g)
 
-        t_bank(4, 0)
-        e1(0)
-        t_bank(4, 1)
-        e1(1)
-        t_bank(4, 2)
-        t_bank(4, 3)
-        load_x(4 + XB)
-        quant(4)
-        t_bank(5, 0)
-        e1(2)
-        t_bank(5, 1)
-        e1(3)
-        t_bank(5, 2)
-        t_bank(5, 3)
-        load_x(5 + XB)
-        h_norms(0)
-
-        for k in range(NP1, NT):
-            for i in E2_LIST[k]:
-                e2(i)
-            if k + 1 < NT:
-                quant(k + 1)
-            for g in range(NG):
-                mx(k, g)
-            for i in E2_LIST[k]:
-                e3(i)
-            if k in H_STEPS:
-                h_norms(H_STEPS[k])
-            if k + 2 < NT:
-                t_bank(k + 2, 0)
-            e1(k)
-            if k + 2 < NT:
-                for b in range(1, 4):
-                    t_bank(k + 2, b)
-                if k + 2 + XB < NT:
-                    load_x(k + 2 + XB)
-        e2(NT - 1)
-        e3(NT - 1)
+        e1v(0)
+        e1s(0)
+        for s in range(NP1, NT + 7):
+            if s < NT:
+                for b in range(4):
+                    t_bank(s, b)
+            if NP1 < s <= NT:
+                quant(s - 1)
+            if 0 < s - 3 < NT:
+                e1v(s - 3)
+            if NP1 <= s - 2 < NT:
+                for g in range(NG):
+                    mx(s - 2, g)
+            if 0 < s - 3 < NT:
+                e1s(s - 3)
+            if 0 <= s - 4 < NT:
+                e2v(s - 4)
+            if 0 <= s - 5 < NT:
+                e2s(s - 5)
+            if s in H_STEPS:
+                h_norms(H_STEPS[s])
+            if 0 <= s - 6 < NT:
+                e3(s - 6)
+            if s + XB < NT:
+                load_x(s + XB)

@@ -28,7 +28,6 @@ C2 = A0 / B0
 
 MANUAL = True
 XB = 8
-NP1 = 4
 
 H_STEPS = {4: 0, 8: 1, 10: 2, 12: 3}
 
@@ -136,16 +135,15 @@ def tile_liquidmemorycell_pb_kernel(tc, x, h, h_candidate, Wd, bd, Wu, bu, out):
 
         wgs = {}
 
-        def w_copy(g):
-            wg = work.tile([P, NOUT, 4], BF16, name="wg", tag="wg", bufs=3, align_bytes=64)
-            wgs[g] = wg
-            for mi in range(2):
-                dst = wg[:, MEM * mi:MEM * (mi + 1), :].rearrange("p (c i) t -> p c t i", i=4)
-                src = wr[mi][:, g].rearrange("p t (c i) -> p c t i", i=4)
-                if mi == 0:
-                    nc.vector.tensor_copy(out=dst, in_=src)
-                else:
-                    nc.scalar.copy(out=dst, in_=src)
+        def w_copy(g, mi, on_vector):
+            if mi == 0:
+                wgs[g] = work.tile([P, NOUT, 4], BF16, name="wg", tag="wg", bufs=3, align_bytes=64)
+            dst = wgs[g][:, MEM * mi:MEM * (mi + 1), :].rearrange("p (c i) t -> p c t i", i=4)
+            src = wr[mi][:, g].rearrange("p t (c i) -> p c t i", i=4)
+            if on_vector:
+                nc.vector.tensor_copy(out=dst, in_=src)
+            else:
+                nc.scalar.copy(out=dst, in_=src)
 
         def w_quant(g):
             nc.vector.quantize_mx(
@@ -215,23 +213,25 @@ def tile_liquidmemorycell_pb_kernel(tc, x, h, h_candidate, Wd, bd, Wu, bu, out):
             rms[i] = rm
 
         def e3(i):
-            o = work.tile([P, MEM], F32, name="o", tag="o", bufs=3)
+            o = work.tile([P, MEM], F32, name="o", tag="o", bufs=8)
             nc.vector.tensor_scalar(out=o[:], in0=ms[i][:], scalar1=rms[i][:, 0:1],
                                     scalar2=hn[:, i:i + 1], op0=ALU.mult, op1=ALU.mult)
             nc.sync.dma_start(out=ov[:, i, :], in_=o[:])
 
-        load_x(0)
-        for n in range(NP1):
-            if n > 0:
-                load_x(n)
-            load_w(2 * n)
-            load_w(2 * n + 1)
         hflat = h.rearrange("(p t) f -> p (t f)", t=NT)
         cflat = h_candidate.rearrange("(p t) f -> p (t f)", t=NT)
-        cut = NP1 * MEM
+        cut = 4 * MEM
+        for i in range(3):
+            load_x(i)
+        for g in range(6):
+            load_w(g)
+        load_x(3)
+        load_w(6)
+        load_w(7)
+        load_x(4)
         nc.sync.dma_start(out=h_all[:, 0:cut], in_=hflat[:, 0:cut])
         nc.sync.dma_start(out=hc_all[:, 0:cut], in_=cflat[:, 0:cut])
-        for i in range(NP1, XB):
+        for i in range(5, XB):
             load_x(i)
         nc.sync.dma_start(out=h_all[:, cut:NT * MEM], in_=hflat[:, cut:NT * MEM])
         nc.sync.dma_start(out=hc_all[:, cut:NT * MEM], in_=cflat[:, cut:NT * MEM])
@@ -241,35 +241,60 @@ def tile_liquidmemorycell_pb_kernel(tc, x, h, h_candidate, Wd, bd, Wu, bu, out):
         nc.vector.tensor_scalar_add(out=bias[:, 0:MEM], in0=bias_ps[:, 0:MEM], scalar1=LNK)
         nc.vector.tensor_copy(out=bias[:, MEM:NOUT], in_=bias_ps[:, MEM:NOUT])
 
-        for n in range(NP1):
+        def transposes(i):
             for b in range(4):
-                t_bank(n, b, on_vector=(b == 3))
-            load_x(n + XB)
-            quant(n)
-            w_copy(2 * n)
-            w_copy(2 * n + 1)
-            w_quant(2 * n)
-            w_quant(2 * n + 1)
-            for g in range(2 * n):
-                mx(n, g)
-            for g in (2 * n, 2 * n + 1):
-                for i in range(n + 1):
+                t_bank(i, b)
+            if i + XB < NT:
+                load_x(i + XB)
+
+        def passes(tiles, gs):
+            for g in gs:
+                for i in tiles:
                     mx(i, g)
 
-        e1v(0)
-        e1s(0)
-        for s in range(NP1, NT + 7):
-            if s < NT:
-                for b in range(4):
-                    t_bank(s, b)
-            if NP1 < s <= NT:
+        transposes(0)
+        transposes(1)
+        quant(0)
+        transposes(2)
+        quant(1)
+        w_copy(0, 0, True)
+        w_copy(0, 1, False)
+        quant(2)
+        w_copy(1, 0, True)
+        w_copy(1, 1, False)
+        w_quant(0)
+        for g in range(2, 6):
+            w_copy(g, 0, True)
+            w_copy(g, 1, False)
+            w_quant(g - 1)
+            passes([0, 1, 2], [g - 2])
+        w_quant(5)
+        passes([0, 1, 2], [4])
+        transposes(3)
+        passes([0, 1, 2], [5])
+        w_copy(6, 0, True)
+        w_copy(6, 1, True)
+        w_copy(7, 0, True)
+        w_quant(6)
+        w_copy(7, 1, True)
+        quant(3)
+        w_quant(7)
+        passes([0, 1, 2], [6])
+        passes([3], [0, 1, 2, 3])
+        transposes(4)
+        passes([0, 1, 2], [7])
+        passes([3], [4, 5, 6, 7])
+
+        for s in range(3, NT + 7):
+            if 5 <= s < NT:
+                transposes(s)
+            if 4 <= s - 1 < NT:
                 quant(s - 1)
-            if 0 < s - 3 < NT:
+            if 0 <= s - 3 < NT:
                 e1v(s - 3)
-            if NP1 <= s - 2 < NT:
-                for g in range(NG):
-                    mx(s - 2, g)
-            if 0 < s - 3 < NT:
+            if 4 <= s - 2 < NT:
+                passes([s - 2], range(NG))
+            if 0 <= s - 3 < NT:
                 e1s(s - 3)
             if 0 <= s - 4 < NT:
                 e2v(s - 4)
@@ -279,5 +304,3 @@ def tile_liquidmemorycell_pb_kernel(tc, x, h, h_candidate, Wd, bd, Wu, bu, out):
                 h_norms(H_STEPS[s])
             if 0 <= s - 6 < NT:
                 e3(s - 6)
-            if s + XB < NT:
-                load_x(s + XB)

@@ -29,8 +29,6 @@ C2 = A0 / B0
 MANUAL = True
 XB = 8
 
-H_STEPS = {4: 0, 8: 1, 10: 2, 12: 3}
-
 
 def tile_liquidmemorycell_pb_kernel(tc, x, h, h_candidate, Wd, bd, Wu, bu, out):
     nc = tc.nc
@@ -87,24 +85,19 @@ def tile_liquidmemorycell_pb_kernel(tc, x, h, h_candidate, Wd, bd, Wu, bu, out):
 
         def load_x(i):
             xt = xpool.tile([P, DIN], BF16, name="xt", tag="xt")
-            head = xt[:, 0:512].rearrange("p (a w f) -> p a w f", a=2, w=2)
-            nc.sync.dma_start(out=head[:, :, 0, :], in_=hv[:, i, :].rearrange("p (a f) -> p a f", a=2))
-            nc.sync.dma_start(out=head[:, :, 1, :], in_=xv[:, i, 0:MEM].rearrange("p (a f) -> p a f", a=2))
-            nc.sync.dma_start(out=xt[:, 512:DIN], in_=xv[:, i, MEM:IN_DIM])
+            nc.sync.dma_start(out=xt[:, 0:MEM], in_=hv[:, i, :])
+            nc.sync.dma_start(out=xt[:, MEM:DIN], in_=xv[:, i, :])
             xs[i] = xt
 
         def load_w(g):
             for mi, w in enumerate((Wd, Wu)):
+                rows = w[512 * g:512 * (g + 1), :]
                 if g == 0:
-                    for hf in range(2):
-                        nc.sync.dma_start(
-                            out=wr[mi][64 * hf:64 * (hf + 1), 0].rearrange("p (u e) n -> p u e n", u=2),
-                            in_=w[MEM * hf:MEM * (hf + 1), :].rearrange("(u p e) n -> p u e n", u=2, e=2),
-                        )
+                    nc.sync.dma_start(out=wr[mi][:, 0], in_=rows.rearrange("(p t) n -> p t n", t=4))
                 else:
                     nc.sync.dma_start(
                         out=wr[mi][:, g].rearrange("p (u e) n -> p u e n", u=2),
-                        in_=w[512 * g:512 * (g + 1), :].rearrange("(u p e) n -> p u e n", u=2, e=2),
+                        in_=rows.rearrange("(u p e) n -> p u e n", u=2, e=2),
                     )
 
         def t_bank(i, b, on_vector=False):
@@ -114,7 +107,8 @@ def tile_liquidmemorycell_pb_kernel(tc, x, h, h_candidate, Wd, bd, Wu, bu, out):
             tp = psum.tile([P, 512], F32, name="tp", tag="tp")
             for s in range(4):
                 j = 4 * b + s
-                nc.tensor.transpose(tp[:, P * s:P * (s + 1)], xw[:, P * j:P * (j + 1)], ident[:])
+                src = xw[:, j:2 * P:2] if j < 2 else xw[:, P * j:P * (j + 1)]
+                nc.tensor.transpose(tp[:, P * s:P * (s + 1)], src, ident[:])
             dst = grp[i][:].bitcast(F32)[:, 512 * b:512 * (b + 1)].rearrange(
                 "p (g r u) -> p g r u", g=2, u=2)
             srcv = tp[:].rearrange("p (g u r) -> p g r u", g=2, u=2)
@@ -166,15 +160,12 @@ def tile_liquidmemorycell_pb_kernel(tc, x, h, h_candidate, Wd, bd, Wu, bu, out):
             )
 
         def h_square(i):
-            nc.scalar.activation(out=junkh[:], in_=h_all[:, MEM * i:MEM * (i + 1)], func=ACT.Square,
+            nc.scalar.activation(out=junkh[:], in_=xs[i][:, 0:MEM], func=ACT.Square,
                                  accum_out=hsq[:, i:i + 1])
-
-        def h_norms(q):
-            cols = slice(4 * q, 4 * q + 4)
-            for i in range(4 * q, 4 * q + 4):
-                h_square(i)
-            nc.gpsimd.tensor_scalar_max(out=hmx[:, cols], in0=hsq[:, cols], scalar1=1e-12)
-            nc.gpsimd.tensor_tensor(out=hn[:, cols], in0=hmx[:, cols], in1=poshalf[:, cols], op=ALU.pow)
+            if i % 4 == 3:
+                cols = slice(i - 3, i + 1)
+                nc.gpsimd.tensor_scalar_max(out=hmx[:, cols], in0=hsq[:, cols], scalar1=1e-12)
+                nc.gpsimd.tensor_tensor(out=hn[:, cols], in0=hmx[:, cols], in1=poshalf[:, cols], op=ALU.pow)
 
         def e1v(i):
             s = work.tile([P, NOUT], F32, name="s", tag="s", bufs=2)
@@ -244,6 +235,7 @@ def tile_liquidmemorycell_pb_kernel(tc, x, h, h_candidate, Wd, bd, Wu, bu, out):
         def transposes(i):
             for b in range(4):
                 t_bank(i, b)
+            h_square(i)
             if i + XB < NT:
                 load_x(i + XB)
 
@@ -300,7 +292,5 @@ def tile_liquidmemorycell_pb_kernel(tc, x, h, h_candidate, Wd, bd, Wu, bu, out):
                 e2v(s - 4)
             if 0 <= s - 5 < NT:
                 e2s(s - 5)
-            if s in H_STEPS:
-                h_norms(H_STEPS[s])
             if 0 <= s - 6 < NT:
                 e3(s - 6)

@@ -86,7 +86,9 @@ def tile_liquidmemorycell_pb_kernel(tc, x, h, h_candidate, Wd, bd, Wu, bu, out):
         def load_x(i):
             xt = xpool.tile([P, DIN], BF16, name="xt", tag="xt")
             nc.sync.dma_start(out=xt[:, 0:MEM], in_=hv[:, i, :])
-            nc.sync.dma_start(out=xt[:, MEM:DIN], in_=xv[:, i, :])
+            cuts = [MEM, 1024, 2048, 3072, DIN] if i == 0 else [MEM, DIN]
+            for lo, hi in zip(cuts[:-1], cuts[1:]):
+                nc.sync.dma_start(out=xt[:, lo:hi], in_=xv[:, i, lo - MEM:hi - MEM])
             xs[i] = xt
 
         def load_w(g):
@@ -120,12 +122,7 @@ def tile_liquidmemorycell_pb_kernel(tc, x, h, h_candidate, Wd, bd, Wu, bu, out):
         def quant(i):
             codes[i] = work.tile([P, NG * P], U32, name="codes", tag="codes", bufs=4, align_bytes=64)
             scl[i] = work.tile([P, NG * P], U8, name="scl", tag="scl", bufs=4, align_bytes=64)
-            for hf in range(2):
-                nc.vector.quantize_mx(
-                    out=codes[i][:, 512 * hf:512 * (hf + 1)].bitcast(FP8X4),
-                    scales=scl[i][:, 512 * hf:512 * (hf + 1)],
-                    in_=grp[i][:, 2048 * hf:2048 * (hf + 1)],
-                )
+            nc.vector.quantize_mx(out=codes[i][:].bitcast(FP8X4), scales=scl[i][:], in_=grp[i][:])
 
         wgs = {}
 
@@ -189,17 +186,17 @@ def tile_liquidmemorycell_pb_kernel(tc, x, h, h_candidate, Wd, bd, Wu, bu, out):
                                            op0=ALU.mult, op1=ALU.subtract)
             w3 = work.tile([P, MEM], F32, name="w3", tag="w3", bufs=2)
             nc.vector.tensor_tensor(out=w3[:], in0=w2[:], in1=gt[:, MEM:NOUT], op=ALU.mult)
-            m = work.tile([P, MEM], F32, name="m", tag="m", bufs=4)
+            m = work.tile([P, MEM], F32, name="m", tag="m", bufs=5)
             nc.vector.tensor_tensor(out=m[:], in0=w3[:], in1=cs, op=ALU.add)
             ms[i] = m
 
         def e2s(i):
             m = ms[i]
-            sm = work.tile([P, 1], F32, name="sm", tag="sm", bufs=4)
+            sm = work.tile([P, 1], F32, name="sm", tag="sm", bufs=5)
             nc.scalar.activation(out=junkm[:], in_=m[:], func=ACT.Square, accum_out=sm[:])
-            sx = work.tile([P, 1], F32, name="sx", tag="sx", bufs=4)
+            sx = work.tile([P, 1], F32, name="sx", tag="sx", bufs=5)
             nc.gpsimd.tensor_scalar_max(out=sx[:], in0=sm[:], scalar1=1e-24)
-            rm = work.tile([P, 1], F32, name="rm", tag="rm", bufs=4)
+            rm = work.tile([P, 1], F32, name="rm", tag="rm", bufs=5)
             nc.gpsimd.tensor_tensor(out=rm[:], in0=sx[:], in1=neghalf[:], op=ALU.pow)
             rms[i] = rm
 
@@ -227,11 +224,6 @@ def tile_liquidmemorycell_pb_kernel(tc, x, h, h_candidate, Wd, bd, Wu, bu, out):
         nc.sync.dma_start(out=h_all[:, cut:NT * MEM], in_=hflat[:, cut:NT * MEM])
         nc.sync.dma_start(out=hc_all[:, cut:NT * MEM], in_=cflat[:, cut:NT * MEM])
 
-        bias_ps = psum.tile([P, NOUT], F32, name="bias_ps", tag="acc")
-        nc.tensor.matmul(out=bias_ps[:], lhsT=ones[:], rhs=brow[:], start=True, stop=True)
-        nc.vector.tensor_scalar_add(out=bias[:, 0:MEM], in0=bias_ps[:, 0:MEM], scalar1=LNK)
-        nc.vector.tensor_copy(out=bias[:, MEM:NOUT], in_=bias_ps[:, MEM:NOUT])
-
         def transposes(i):
             for b in range(4):
                 t_bank(i, b)
@@ -249,6 +241,10 @@ def tile_liquidmemorycell_pb_kernel(tc, x, h, h_candidate, Wd, bd, Wu, bu, out):
         quant(0)
         transposes(2)
         quant(1)
+        bias_ps = psum.tile([P, NOUT], F32, name="bias_ps", tag="acc")
+        nc.tensor.matmul(out=bias_ps[:], lhsT=ones[:], rhs=brow[:], start=True, stop=True)
+        nc.vector.tensor_scalar_add(out=bias[:, 0:MEM], in0=bias_ps[:, 0:MEM], scalar1=LNK)
+        nc.vector.tensor_copy(out=bias[:, MEM:NOUT], in_=bias_ps[:, MEM:NOUT])
         w_copy(0, 0, True)
         w_copy(0, 1, False)
         quant(2)
@@ -277,7 +273,7 @@ def tile_liquidmemorycell_pb_kernel(tc, x, h, h_candidate, Wd, bd, Wu, bu, out):
         passes([0, 1, 2], [7])
         passes([3], [4, 5, 6, 7])
 
-        for s in range(3, NT + 7):
+        for s in range(3, NT + 8):
             if 5 <= s < NT:
                 transposes(s)
             if 4 <= s - 1 < NT:
@@ -292,5 +288,5 @@ def tile_liquidmemorycell_pb_kernel(tc, x, h, h_candidate, Wd, bd, Wu, bu, out):
                 e2v(s - 4)
             if 0 <= s - 5 < NT:
                 e2s(s - 5)
-            if 0 <= s - 6 < NT:
-                e3(s - 6)
+            if 0 <= s - 7 < NT:
+                e3(s - 7)

@@ -28,6 +28,9 @@ C2 = A0 / B0
 
 MANUAL = True
 XB = 8
+NH = 4
+ORDER = "x0 x1 x2 x3 w0 w1 w2 w3 w4 w5 w6 w7"
+SHARE = (0, 1)
 
 
 def tile_liquidmemorycell_pb_kernel(tc, x, h, h_candidate, Wd, bd, Wu, bu, out):
@@ -61,7 +64,6 @@ def tile_liquidmemorycell_pb_kernel(tc, x, h, h_candidate, Wd, bd, Wu, bu, out):
         poshalf = const.tile([P, NT], F32, name="poshalf")
         nc.gpsimd.memset(poshalf[:], 0.5)
 
-        h_all = const.tile([P, NT * MEM], BF16, name="h_all")
         hc_all = const.tile([P, NT * MEM], BF16, name="hc_all")
         wr = [const.tile([P, NG, 4, MEM], BF16, name="wr%d" % mi) for mi in range(2)]
         wcodes = const.tile([P, NG * NOUT], U32, name="wcodes", align_bytes=64)
@@ -119,10 +121,14 @@ def tile_liquidmemorycell_pb_kernel(tc, x, h, h_candidate, Wd, bd, Wu, bu, out):
             else:
                 nc.scalar.copy(out=dst, in_=srcv)
 
-        def quant(i):
-            codes[i] = work.tile([P, NG * P], U32, name="codes", tag="codes", bufs=4, align_bytes=64)
-            scl[i] = work.tile([P, NG * P], U8, name="scl", tag="scl", bufs=4, align_bytes=64)
-            nc.vector.quantize_mx(out=codes[i][:].bitcast(FP8X4), scales=scl[i][:], in_=grp[i][:])
+        def quant(i, half=None):
+            if half in (None, 0):
+                codes[i] = work.tile([P, NG * P], U32, name="codes", tag="codes", bufs=4, align_bytes=64)
+                scl[i] = work.tile([P, NG * P], U8, name="scl", tag="scl", bufs=4, align_bytes=64)
+            w = NG * P // 2
+            cols = slice(0, 2 * w) if half is None else slice(w * half, w * (half + 1))
+            nc.vector.quantize_mx(out=codes[i][:, cols].bitcast(FP8X4), scales=scl[i][:, cols],
+                                  in_=grp[i][:, 4 * cols.start:4 * cols.stop])
 
         wgs = {}
 
@@ -143,17 +149,21 @@ def tile_liquidmemorycell_pb_kernel(tc, x, h, h_candidate, Wd, bd, Wu, bu, out):
                 in_=wgs[g][:].rearrange("p n t -> p (n t)"),
             )
 
+        npass = {}
+
         def mx(i, g):
-            if g == 0:
+            if i not in npass:
+                npass[i] = 0
                 acc[i] = psum.tile([P, NOUT], F32, name="acc", tag="acc")
+            npass[i] += 1
             nc.tensor.matmul_mx(
                 out=acc[i][:],
                 lhsT=codes[i][:, P * g:P * (g + 1)].bitcast(FP8X4),
                 lhsT_scale=scl[i][:, P * g:P * (g + 1)],
                 rhs=wcodes[:, NOUT * g:NOUT * (g + 1)].bitcast(FP8X4),
                 rhs_scale=wscl[:, NOUT * g:NOUT * (g + 1)],
-                start=(g == 0),
-                stop=(g == NG - 1),
+                start=(npass[i] == 1),
+                stop=(npass[i] == NG),
             )
 
         def h_square(i):
@@ -164,31 +174,46 @@ def tile_liquidmemorycell_pb_kernel(tc, x, h, h_candidate, Wd, bd, Wu, bu, out):
                 nc.gpsimd.tensor_scalar_max(out=hmx[:, cols], in0=hsq[:, cols], scalar1=1e-12)
                 nc.gpsimd.tensor_tensor(out=hn[:, cols], in0=hmx[:, cols], in1=poshalf[:, cols], op=ALU.pow)
 
-        def e1v(i):
-            s = work.tile([P, NOUT], F32, name="s", tag="s", bufs=2)
-            nc.vector.tensor_tensor(out=s[:], in0=acc[i][:], in1=bias[:], op=ALU.add)
-            ss[i] = s
+        def e1v_full(i):
+            ss[i] = work.tile([P, NOUT], F32, name="s", tag="s", bufs=3)
+            nc.vector.tensor_tensor(out=ss[i][:], in0=acc[i][:], in1=bias[:], op=ALU.add)
 
-        def e1s(i):
-            gt = work.tile([P, NOUT], F32, name="gt", tag="gt", bufs=3)
-            nc.scalar.activation(out=gt[:], in_=ss[i][:], func=ACT.Sigmoid, scale=-1.0)
-            gts[i] = gt
+        def e1v(i, half):
+            if half == 0:
+                ss[i] = work.tile([P, NOUT], F32, name="s", tag="s", bufs=3)
+            cols = slice(MEM * half, MEM * (half + 1))
+            nc.vector.tensor_tensor(out=ss[i][:, cols], in0=acc[i][:, cols], in1=bias[:, cols], op=ALU.add)
 
-        def e2v(i):
-            hs = h_all[:, MEM * i:MEM * (i + 1)]
+        def e1s(i, half=None):
+            if half in (None, 0):
+                gts[i] = work.tile([P, NOUT], F32, name="gt", tag="gt", bufs=3)
+            cols = slice(0, NOUT) if half is None else slice(MEM * half, MEM * (half + 1))
+            nc.scalar.activation(out=gts[i][:, cols], in_=ss[i][:, cols], func=ACT.Sigmoid, scale=-1.0)
+
+        ws = {}
+
+        def e2v(i, step):
+            hs = xs[i][:, 0:MEM]
             cs = hc_all[:, MEM * i:MEM * (i + 1)]
             gt = gts[i]
-            w1 = work.tile([P, MEM], F32, name="w1", tag="w1", bufs=2)
-            nc.vector.scalar_tensor_tensor(out=w1[:], in0=gt[:, 0:MEM], scalar=C2, in1=hs,
-                                           op0=ALU.add, op1=ALU.mult)
-            w2 = work.tile([P, MEM], F32, name="w2", tag="w2", bufs=2)
-            nc.vector.scalar_tensor_tensor(out=w2[:], in0=w1[:], scalar=BETA, in1=cs,
-                                           op0=ALU.mult, op1=ALU.subtract)
-            w3 = work.tile([P, MEM], F32, name="w3", tag="w3", bufs=2)
-            nc.vector.tensor_tensor(out=w3[:], in0=w2[:], in1=gt[:, MEM:NOUT], op=ALU.mult)
-            m = work.tile([P, MEM], F32, name="m", tag="m", bufs=5)
-            nc.vector.tensor_tensor(out=m[:], in0=w3[:], in1=cs, op=ALU.add)
-            ms[i] = m
+            if step == 0:
+                w1 = work.tile([P, MEM], F32, name="w1", tag="w1", bufs=2)
+                nc.vector.scalar_tensor_tensor(out=w1[:], in0=gt[:, 0:MEM], scalar=C2, in1=hs,
+                                               op0=ALU.add, op1=ALU.mult)
+                ws[i] = w1
+            elif step == 1:
+                w2 = work.tile([P, MEM], F32, name="w2", tag="w2", bufs=2)
+                nc.vector.scalar_tensor_tensor(out=w2[:], in0=ws[i][:], scalar=BETA, in1=cs,
+                                               op0=ALU.mult, op1=ALU.subtract)
+                ws[i] = w2
+            elif step == 2:
+                w3 = work.tile([P, MEM], F32, name="w3", tag="w3", bufs=2)
+                nc.vector.tensor_tensor(out=w3[:], in0=ws[i][:], in1=gt[:, MEM:NOUT], op=ALU.mult)
+                ws[i] = w3
+            else:
+                m = work.tile([P, MEM], F32, name="m", tag="m", bufs=5)
+                nc.vector.tensor_tensor(out=m[:], in0=ws[i][:], in1=cs, op=ALU.add)
+                ms[i] = m
 
         def e2s(i):
             m = ms[i]
@@ -206,87 +231,86 @@ def tile_liquidmemorycell_pb_kernel(tc, x, h, h_candidate, Wd, bd, Wu, bu, out):
                                     scalar2=hn[:, i:i + 1], op0=ALU.mult, op1=ALU.mult)
             nc.sync.dma_start(out=ov[:, i, :], in_=o[:])
 
-        hflat = h.rearrange("(p t) f -> p (t f)", t=NT)
         cflat = h_candidate.rearrange("(p t) f -> p (t f)", t=NT)
         cut = 4 * MEM
-        for i in range(3):
-            load_x(i)
-        for g in range(6):
-            load_w(g)
-        load_x(3)
-        load_w(6)
-        load_w(7)
-        load_x(4)
-        nc.sync.dma_start(out=h_all[:, 0:cut], in_=hflat[:, 0:cut])
+        order = [(o[0], int(o[1:])) for o in ORDER.split()]
+        for kind, j in order:
+            if kind == "x":
+                load_x(j)
+            else:
+                load_w(j)
+        nx = 1 + max([j for kind, j in order if kind == "x"])
         nc.sync.dma_start(out=hc_all[:, 0:cut], in_=cflat[:, 0:cut])
-        for i in range(5, XB):
+        for i in range(nx, XB):
             load_x(i)
-        nc.sync.dma_start(out=h_all[:, cut:NT * MEM], in_=hflat[:, cut:NT * MEM])
         nc.sync.dma_start(out=hc_all[:, cut:NT * MEM], in_=cflat[:, cut:NT * MEM])
 
         def transposes(i):
             for b in range(4):
-                t_bank(i, b)
+                t_bank(i, b, on_vector=(i in SHARE and b % 2 == 1))
             h_square(i)
-            if i + XB < NT:
-                load_x(i + XB)
 
         def passes(tiles, gs):
             for g in gs:
                 for i in tiles:
                     mx(i, g)
 
-        transposes(0)
-        transposes(1)
-        quant(0)
-        transposes(2)
-        quant(1)
-        bias_ps = psum.tile([P, NOUT], F32, name="bias_ps", tag="acc")
-        nc.tensor.matmul(out=bias_ps[:], lhsT=ones[:], rhs=brow[:], start=True, stop=True)
-        nc.vector.tensor_scalar_add(out=bias[:, 0:MEM], in0=bias_ps[:, 0:MEM], scalar1=LNK)
-        nc.vector.tensor_copy(out=bias[:, MEM:NOUT], in_=bias_ps[:, MEM:NOUT])
-        w_copy(0, 0, True)
-        w_copy(0, 1, False)
-        quant(2)
-        w_copy(1, 0, True)
-        w_copy(1, 1, False)
-        w_quant(0)
-        for g in range(2, 6):
-            w_copy(g, 0, True)
-            w_copy(g, 1, False)
-            w_quant(g - 1)
-            passes([0, 1, 2], [g - 2])
-        w_quant(5)
-        passes([0, 1, 2], [4])
-        transposes(3)
-        passes([0, 1, 2], [5])
-        w_copy(6, 0, True)
-        w_copy(6, 1, True)
-        w_copy(7, 0, True)
-        w_quant(6)
-        w_copy(7, 1, True)
-        quant(3)
-        w_quant(7)
-        passes([0, 1, 2], [6])
-        passes([3], [0, 1, 2, 3])
-        transposes(4)
-        passes([0, 1, 2], [7])
-        passes([3], [4, 5, 6, 7])
+        def ok(i):
+            return 0 <= i < NT
+
+        xq = []
+        wq = []
+        n = len(order)
+        for kslot in range(n + 2):
+            if kslot < n:
+                kind, j = order[kslot]
+                if kind == "x":
+                    transposes(j)
+                else:
+                    w_copy(j, 0, True)
+                    w_copy(j, 1, False)
+            if kslot >= 2:
+                kind, j = order[kslot - 2]
+                if kind == "x" and j < NH:
+                    passes([j], wq)
+                    xq.append(j)
+                elif kind == "w":
+                    passes(xq, [j])
+                    wq.append(j)
+            if 1 <= kslot <= n:
+                kind, j = order[kslot - 1]
+                if kind == "x":
+                    quant(j)
+                else:
+                    w_quant(j)
+            if kslot == 0:
+                bias_ps = psum.tile([P, NOUT], F32, name="bias_ps", tag="acc")
+                nc.tensor.matmul(out=bias_ps[:], lhsT=ones[:], rhs=brow[:], start=True, stop=True)
+                nc.vector.tensor_scalar_add(out=bias[:, 0:MEM], in0=bias_ps[:, 0:MEM], scalar1=LNK)
+                nc.vector.tensor_copy(out=bias[:, MEM:NOUT], in_=bias_ps[:, MEM:NOUT])
 
         for s in range(3, NT + 8):
-            if 5 <= s < NT:
-                transposes(s)
-            if 4 <= s - 1 < NT:
+            if nx <= s - 1 < NT:
                 quant(s - 1)
-            if 0 <= s - 3 < NT:
-                e1v(s - 3)
-            if 4 <= s - 2 < NT:
+            if nx <= s < NT:
+                transposes(s)
+            if ok(s - 4):
+                e2v(s - 4, 0)
+            if ok(s - 3):
+                e1v_full(s - 3)
+            if ok(s - 4):
+                e2v(s - 4, 1)
+            if NH <= s - 2 < NT:
                 passes([s - 2], range(NG))
-            if 0 <= s - 3 < NT:
+            if ok(s - 3):
                 e1s(s - 3)
-            if 0 <= s - 4 < NT:
-                e2v(s - 4)
-            if 0 <= s - 5 < NT:
-                e2s(s - 5)
-            if 0 <= s - 7 < NT:
+            if ok(s - 7):
                 e3(s - 7)
+            if ok(s - 4):
+                e2v(s - 4, 2)
+            if ok(s - 4):
+                e2v(s - 4, 3)
+                if s - 4 + XB < NT:
+                    load_x(s - 4 + XB)
+            if ok(s - 5):
+                e2s(s - 5)

@@ -31,6 +31,8 @@ XB = 8
 NH = 4
 ORDER = "x0 x1 x2 x3 w0 w1 w2 w3 w4 w5 w6 w7"
 SHARE = (0, 1)
+LATE_NORM = (2, 3)
+CB = 4
 
 
 def tile_liquidmemorycell_pb_kernel(tc, x, h, h_candidate, Wd, bd, Wu, bu, out):
@@ -39,7 +41,13 @@ def tile_liquidmemorycell_pb_kernel(tc, x, h, h_candidate, Wd, bd, Wu, bu, out):
         const = ctx.enter_context(tc.tile_pool(name="const", bufs=1))
         xpool = ctx.enter_context(tc.tile_pool(name="xpool", bufs=XB))
         work = ctx.enter_context(tc.tile_pool(name="work", bufs=2))
-        psum = ctx.enter_context(tc.psum_pool(name="psum", bufs=4))
+        psum = ctx.enter_context(tc.psum_pool(name="psum", bufs=1))
+        free_banks = list(range(8))
+
+        def take_bank(name, shape, dtype):
+            b = free_banks[0]
+            free_banks.remove(b)
+            return b, psum.tile(shape, dtype, name=name, tag="bank%d" % b)
         if MANUAL:
             ctx.enter_context(tc.manual_schedule())
 
@@ -108,7 +116,7 @@ def tile_liquidmemorycell_pb_kernel(tc, x, h, h_candidate, Wd, bd, Wu, bu, out):
             if b == 0:
                 grp[i] = work.tile([P, DIN], BF16, name="grp", tag="grp", bufs=3, align_bytes=64)
             xw = xs[i][:].bitcast(F32)
-            tp = psum.tile([P, 512], F32, name="tp", tag="tp")
+            bno, tp = take_bank("tp", [P, 512], F32)
             for s in range(4):
                 j = 4 * b + s
                 src = xw[:, j:2 * P:2] if j < 2 else xw[:, P * j:P * (j + 1)]
@@ -120,11 +128,12 @@ def tile_liquidmemorycell_pb_kernel(tc, x, h, h_candidate, Wd, bd, Wu, bu, out):
                 nc.vector.tensor_copy(out=dst, in_=srcv)
             else:
                 nc.scalar.copy(out=dst, in_=srcv)
+            free_banks.append(bno)
 
         def quant(i, half=None):
             if half in (None, 0):
-                codes[i] = work.tile([P, NG * P], U32, name="codes", tag="codes", bufs=4, align_bytes=64)
-                scl[i] = work.tile([P, NG * P], U8, name="scl", tag="scl", bufs=4, align_bytes=64)
+                codes[i] = work.tile([P, NG * P], U32, name="codes", tag="codes", bufs=CB, align_bytes=64)
+                scl[i] = work.tile([P, NG * P], U8, name="scl", tag="scl", bufs=CB, align_bytes=64)
             w = NG * P // 2
             cols = slice(0, 2 * w) if half is None else slice(w * half, w * (half + 1))
             nc.vector.quantize_mx(out=codes[i][:, cols].bitcast(FP8X4), scales=scl[i][:, cols],
@@ -150,11 +159,12 @@ def tile_liquidmemorycell_pb_kernel(tc, x, h, h_candidate, Wd, bd, Wu, bu, out):
             )
 
         npass = {}
+        accb = {}
 
         def mx(i, g):
             if i not in npass:
                 npass[i] = 0
-                acc[i] = psum.tile([P, NOUT], F32, name="acc", tag="acc")
+                accb[i], acc[i] = take_bank("acc", [P, NOUT], F32)
             npass[i] += 1
             nc.tensor.matmul_mx(
                 out=acc[i][:],
@@ -177,6 +187,7 @@ def tile_liquidmemorycell_pb_kernel(tc, x, h, h_candidate, Wd, bd, Wu, bu, out):
         def e1v_full(i):
             ss[i] = work.tile([P, NOUT], F32, name="s", tag="s", bufs=3)
             nc.vector.tensor_tensor(out=ss[i][:], in0=acc[i][:], in1=bias[:], op=ALU.add)
+            free_banks.append(accb[i])
 
         def e1v(i, half):
             if half == 0:
@@ -248,7 +259,8 @@ def tile_liquidmemorycell_pb_kernel(tc, x, h, h_candidate, Wd, bd, Wu, bu, out):
         def transposes(i):
             for b in range(4):
                 t_bank(i, b, on_vector=(i in SHARE and b % 2 == 1))
-            h_square(i)
+            if i not in LATE_NORM:
+                h_square(i)
 
         def passes(tiles, gs):
             for g in gs:
@@ -284,10 +296,14 @@ def tile_liquidmemorycell_pb_kernel(tc, x, h, h_candidate, Wd, bd, Wu, bu, out):
                 else:
                     w_quant(j)
             if kslot == 0:
-                bias_ps = psum.tile([P, NOUT], F32, name="bias_ps", tag="acc")
+                bb, bias_ps = take_bank("bias_ps", [P, NOUT], F32)
                 nc.tensor.matmul(out=bias_ps[:], lhsT=ones[:], rhs=brow[:], start=True, stop=True)
                 nc.vector.tensor_scalar_add(out=bias[:, 0:MEM], in0=bias_ps[:, 0:MEM], scalar1=LNK)
                 nc.vector.tensor_copy(out=bias[:, MEM:NOUT], in_=bias_ps[:, MEM:NOUT])
+                free_banks.append(bb)
+
+        for i in LATE_NORM:
+            h_square(i)
 
         for s in range(3, NT + 8):
             if nx <= s - 1 < NT:

@@ -31,6 +31,7 @@ XB = 8
 NH = 4
 ORDER = "x0 x1 x2 x3 w0 w1 w2 w3 w4 w5 w6 w7"
 SHARE = (0, 1)
+NWARM = 8
 LATE_NORM = (2, 3)
 CB = 4
 
@@ -278,6 +279,11 @@ def tile_liquidmemorycell_pb_kernel(tc, x, h, h_candidate, Wd, bd, Wu, bu, out):
                 kind, j = order[kslot]
                 if kind == "x":
                     transposes(j)
+                    if j == NH - 1:
+                        wb, wps = take_bank("warmup", [P, NOUT], F32)
+                        for r in range(NWARM):
+                            nc.tensor.matmul(out=wps[:], lhsT=ones[:], rhs=brow[:], start=True, stop=True)
+                        free_banks.append(wb)
                 else:
                     w_copy(j, 0, True)
                     w_copy(j, 1, False)

@@ -31,7 +31,7 @@ XB = 8
 NH = 4
 ORDER = "x0 x1 x2 x3 w0 w1 w2 w3 w4 w5 w6 w7"
 SHARE = (0, 1)
-NWARM = 8
+NWARM = (2, 2, 2, 12)
 LATE_NORM = (2, 3)
 CB = 4
 
@@ -279,9 +279,9 @@ def tile_liquidmemorycell_pb_kernel(tc, x, h, h_candidate, Wd, bd, Wu, bu, out):
                 kind, j = order[kslot]
                 if kind == "x":
                     transposes(j)
-                    if j == NH - 1:
+                    if j < NH:
                         wb, wps = take_bank("warmup", [P, NOUT], F32)
-                        for r in range(NWARM):
+                        for r in range(NWARM[j]):
                             nc.tensor.matmul(out=wps[:], lhsT=ones[:], rhs=brow[:], start=True, stop=True)
                         free_banks.append(wb)
                 else:

@@ -31,6 +31,7 @@ XB = 8
 NH = 4
 ORDER = "x0 x1 x2 x3 w0 w1 w2 w3 w4 w5 w6 w7"
 SHARE = (0, 1)
+NBATCH = 12
 NWARM = (2, 2, 2, 12)
 LATE_NORM = (2, 3)
 CB = 4
@@ -68,7 +69,7 @@ def tile_liquidmemorycell_pb_kernel(tc, x, h, h_candidate, Wd, bd, Wu, bu, out):
         nc.vector.memset(warm[:], 0.0)
         warm2 = const.tile([P, 1], F32, name="warm2")
         nc.scalar.activation(out=warm2[:], in_=warm[:], func=ACT.Sigmoid)
-        neghalf = const.tile([P, 1], F32, name="neghalf")
+        neghalf = const.tile([P, 4], F32, name="neghalf")
         nc.gpsimd.memset(neghalf[:], -0.5)
         poshalf = const.tile([P, NT], F32, name="poshalf")
         nc.gpsimd.memset(poshalf[:], 0.5)
@@ -223,23 +224,30 @@ def tile_liquidmemorycell_pb_kernel(tc, x, h, h_candidate, Wd, bd, Wu, bu, out):
                 nc.vector.tensor_tensor(out=w3[:], in0=ws[i][:], in1=gt[:, MEM:NOUT], op=ALU.mult)
                 ws[i] = w3
             else:
-                m = work.tile([P, MEM], F32, name="m", tag="m", bufs=5)
+                m = work.tile([P, MEM], F32, name="m", tag="m", bufs=8)
                 nc.vector.tensor_tensor(out=m[:], in0=ws[i][:], in1=cs, op=ALU.add)
                 ms[i] = m
 
+        smq = {}
+
         def e2s(i):
             m = ms[i]
-            sm = work.tile([P, 1], F32, name="sm", tag="sm", bufs=5)
-            nc.scalar.activation(out=junkm[:], in_=m[:], func=ACT.Square, accum_out=sm[:])
-            sx = work.tile([P, 1], F32, name="sx", tag="sx", bufs=5)
-            nc.gpsimd.tensor_scalar_max(out=sx[:], in0=sm[:], scalar1=1e-24)
-            rm = work.tile([P, 1], F32, name="rm", tag="rm", bufs=5)
-            nc.gpsimd.tensor_tensor(out=rm[:], in0=sx[:], in1=neghalf[:], op=ALU.pow)
-            rms[i] = rm
+            n = 4 if i < NBATCH else 1
+            b, j = (i // n, i % n)
+            if j == 0:
+                smq[b] = work.tile([P, n], F32, name="sm", tag="sm%d" % n, bufs=4)
+            nc.scalar.activation(out=junkm[:], in_=m[:], func=ACT.Square, accum_out=smq[b][:, j:j + 1])
+            if j == n - 1:
+                sx = work.tile([P, n], F32, name="sx", tag="sx%d" % n, bufs=4)
+                nc.gpsimd.tensor_scalar_max(out=sx[:], in0=smq[b][:], scalar1=1e-24)
+                rm = work.tile([P, n], F32, name="rm", tag="rm%d" % n, bufs=4)
+                nc.gpsimd.tensor_tensor(out=rm[:], in0=sx[:], in1=neghalf[:, 0:n], op=ALU.pow)
+                for k in range(n):
+                    rms[i - n + 1 + k] = rm[:, k:k + 1]
 
         def e3(i):
             o = work.tile([P, MEM], F32, name="o", tag="o", bufs=8)
-            nc.vector.tensor_scalar(out=o[:], in0=ms[i][:], scalar1=rms[i][:, 0:1],
+            nc.vector.tensor_scalar(out=o[:], in0=ms[i][:], scalar1=rms[i],
                                     scalar2=hn[:, i:i + 1], op0=ALU.mult, op1=ALU.mult)
             nc.sync.dma_start(out=ov[:, i, :], in_=o[:])
 
@@ -326,8 +334,9 @@ def tile_liquidmemorycell_pb_kernel(tc, x, h, h_candidate, Wd, bd, Wu, bu, out):
                 passes([s - 2], range(NG))
             if ok(s - 3):
                 e1s(s - 3)
-            if ok(s - 7):
-                e3(s - 7)
+            for i in ([s - 10] if s - 10 < NBATCH else []) + ([s - 7] if s - 7 >= NBATCH else []):
+                if ok(i):
+                    e3(i)
             if ok(s - 4):
                 e2v(s - 4, 2)
             if ok(s - 4):

@@ -32,8 +32,10 @@ NH = 4
 ORDER = "x0 x1 x2 x3 w0 w1 w2 w3 w4 w5 w6 w7"
 SHARE = (0, 1)
 NBATCH = 12
+ROOTS = (0, 4, 8, 12, 15)
+HB = 8
 NWARM = (2, 2, 2, 12)
-LATE_NORM = (2, 3)
+LATE_NORM = (2, 3, 4, 5)
 CB = 4
 
 
@@ -181,8 +183,8 @@ def tile_liquidmemorycell_pb_kernel(tc, x, h, h_candidate, Wd, bd, Wu, bu, out):
         def h_square(i):
             nc.scalar.activation(out=junkh[:], in_=xs[i][:, 0:MEM], func=ACT.Square,
                                  accum_out=hsq[:, i:i + 1])
-            if i % 4 == 3:
-                cols = slice(i - 3, i + 1)
+            if i % HB == HB - 1:
+                cols = slice(i - HB + 1, i + 1)
                 nc.gpsimd.tensor_scalar_max(out=hmx[:, cols], in0=hsq[:, cols], scalar1=1e-12)
                 nc.gpsimd.tensor_tensor(out=hn[:, cols], in0=hmx[:, cols], in1=poshalf[:, cols], op=ALU.pow)
 
@@ -232,8 +234,9 @@ def tile_liquidmemorycell_pb_kernel(tc, x, h, h_candidate, Wd, bd, Wu, bu, out):
 
         def e2s(i):
             m = ms[i]
-            n = 4 if i < NBATCH else 1
-            b, j = (i // n, i % n)
+            first = max([f for f in ROOTS if f <= i])
+            n = min([f for f in ROOTS + (NT,) if f > i]) - first
+            b, j = (first, i - first)
             if j == 0:
                 smq[b] = work.tile([P, n], F32, name="sm", tag="sm%d" % n, bufs=4)
             nc.scalar.activation(out=junkm[:], in_=m[:], func=ACT.Square, accum_out=smq[b][:, j:j + 1])
@@ -334,8 +337,10 @@ def tile_liquidmemorycell_pb_kernel(tc, x, h, h_candidate, Wd, bd, Wu, bu, out):
                 passes([s - 2], range(NG))
             if ok(s - 3):
                 e1s(s - 3)
-            for i in ([s - 10] if s - 10 < NBATCH else []) + ([s - 7] if s - 7 >= NBATCH else []):
-                if ok(i):
+            for i in range(NT):
+                first = max([f for f in ROOTS if f <= i])
+                last = min([f for f in ROOTS + (NT,) if f > i]) - 1
+                if s == last + 7 + (i - first if i < NBATCH else 0):
                     e3(i)
             if ok(s - 4):
                 e2v(s - 4, 2)

@@ -189,7 +189,7 @@ def tile_liquidmemorycell_pb_kernel(tc, x, h, h_candidate, Wd, bd, Wu, bu, out):
                 nc.gpsimd.tensor_tensor(out=hn[:, cols], in0=hmx[:, cols], in1=poshalf[:, cols], op=ALU.pow)
 
         def e1v_full(i):
-            ss[i] = work.tile([P, NOUT], F32, name="s", tag="s", bufs=3)
+            ss[i] = work.tile([P, NOUT], F32, name="s", tag="s", bufs=5)
             nc.vector.tensor_tensor(out=ss[i][:], in0=acc[i][:], in1=bias[:], op=ALU.add)
             free_banks.append(accb[i])
 
@@ -329,8 +329,9 @@ def tile_liquidmemorycell_pb_kernel(tc, x, h, h_candidate, Wd, bd, Wu, bu, out):
                 transposes(s)
             if ok(s - 4):
                 e2v(s - 4, 0)
-            if ok(s - 3):
-                e1v_full(s - 3)
+            for i in (range(NH) if s == 3 else [s - 3]):
+                if ok(i) and (s == 3 or i >= NH):
+                    e1v_full(i)
             if ok(s - 4):
                 e2v(s - 4, 1)
             if NH <= s - 2 < NT:

@@ -37,6 +37,9 @@ HB = 8
 NWARM = (2, 2, 2, 12)
 LATE_NORM = (2, 3, 4, 5)
 CB = 4
+QW = 1
+QS = 9
+QE = 15
 
 
 def tile_liquidmemorycell_pb_kernel(tc, x, h, h_candidate, Wd, bd, Wu, bu, out):
@@ -323,8 +326,9 @@ def tile_liquidmemorycell_pb_kernel(tc, x, h, h_candidate, Wd, bd, Wu, bu, out):
             h_square(i)
 
         for s in range(3, NT + 8):
-            if nx <= s - 1 < NT:
-                quant(s - 1)
+            q = s - 1
+            if nx <= q < NT and (QW == 0 or s < QS or s >= QE):
+                quant(q)
             if nx <= s < NT:
                 transposes(s)
             if ok(s - 4):
@@ -334,6 +338,8 @@ def tile_liquidmemorycell_pb_kernel(tc, x, h, h_candidate, Wd, bd, Wu, bu, out):
                     e1v_full(i)
             if ok(s - 4):
                 e2v(s - 4, 1)
+            if nx <= q < NT and QW == 2 and QS <= s < QE:
+                quant(q, 0)
             if NH <= s - 2 < NT:
                 passes([s - 2], range(NG))
             if ok(s - 3):
@@ -345,6 +351,10 @@ def tile_liquidmemorycell_pb_kernel(tc, x, h, h_candidate, Wd, bd, Wu, bu, out):
                     e3(i)
             if ok(s - 4):
                 e2v(s - 4, 2)
+            if nx <= q < NT and QW == 1 and QS <= s < QE:
+                quant(q)
+            if nx <= q < NT and QW == 2 and QS <= s < QE:
+                quant(q, 1)
             if ok(s - 4):
                 e2v(s - 4, 3)
                 if s - 4 + XB < NT:

@@ -30,7 +30,7 @@ MANUAL = True
 XB = 8
 NH = 4
 ORDER = "x0 x1 x2 x3 w0 w1 w2 w3 w4 w5 w6 w7"
-SHARE = (0, 1)
+SHARE = (0, 1, 4)
 NBATCH = 12
 ROOTS = (0, 4, 8, 12, 15)
 HB = 8
@@ -40,6 +40,10 @@ CB = 4
 QW = 1
 QS = 9
 QE = 15
+G1 = 3
+B1 = 5
+HCP = 7
+EV = 99
 
 
 def tile_liquidmemorycell_pb_kernel(tc, x, h, h_candidate, Wd, bd, Wu, bu, out):
@@ -119,6 +123,13 @@ def tile_liquidmemorycell_pb_kernel(tc, x, h, h_candidate, Wd, bd, Wu, bu, out):
                         in_=rows.rearrange("(u p e) n -> p u e n", u=2, e=2),
                     )
 
+        evens = {}
+
+        def spread_pass0(i):
+            evens[i] = work.tile([P, 2 * P], F32, name="even", tag="even", bufs=2)
+            nc.vector.tensor_copy(out=evens[i][:].rearrange("p (u w) -> p u w", u=2),
+                                  in_=xs[i][:, 0:4 * P].bitcast(F32).rearrange("p (w u) -> p u w", u=2))
+
         def t_bank(i, b, on_vector=False):
             if b == 0:
                 grp[i] = work.tile([P, DIN], BF16, name="grp", tag="grp", bufs=3, align_bytes=64)
@@ -126,7 +137,12 @@ def tile_liquidmemorycell_pb_kernel(tc, x, h, h_candidate, Wd, bd, Wu, bu, out):
             bno, tp = take_bank("tp", [P, 512], F32)
             for s in range(4):
                 j = 4 * b + s
-                src = xw[:, j:2 * P:2] if j < 2 else xw[:, P * j:P * (j + 1)]
+                if j >= 2:
+                    src = xw[:, P * j:P * (j + 1)]
+                elif i in evens:
+                    src = evens[i][:, P * j:P * (j + 1)]
+                else:
+                    src = xw[:, j:2 * P:2]
                 nc.tensor.transpose(tp[:, P * s:P * (s + 1)], src, ident[:])
             dst = grp[i][:].bitcast(F32)[:, 512 * b:512 * (b + 1)].rearrange(
                 "p (g r u) -> p g r u", g=2, u=2)
@@ -204,7 +220,7 @@ def tile_liquidmemorycell_pb_kernel(tc, x, h, h_candidate, Wd, bd, Wu, bu, out):
 
         def e1s(i, half=None):
             if half in (None, 0):
-                gts[i] = work.tile([P, NOUT], F32, name="gt", tag="gt", bufs=3)
+                gts[i] = work.tile([P, NOUT], F32, name="gt", tag="gt", bufs=4)
             cols = slice(0, NOUT) if half is None else slice(MEM * half, MEM * (half + 1))
             nc.scalar.activation(out=gts[i][:, cols], in_=ss[i][:, cols], func=ACT.Sigmoid, scale=-1.0)
 
@@ -266,8 +282,10 @@ def tile_liquidmemorycell_pb_kernel(tc, x, h, h_candidate, Wd, bd, Wu, bu, out):
             else:
                 load_w(j)
         nx = 1 + max([j for kind, j in order if kind == "x"])
+        for i in range(nx, HCP):
+            load_x(i)
         nc.sync.dma_start(out=hc_all[:, 0:cut], in_=cflat[:, 0:cut])
-        for i in range(nx, XB):
+        for i in range(HCP, XB):
             load_x(i)
         nc.sync.dma_start(out=hc_all[:, cut:NT * MEM], in_=cflat[:, cut:NT * MEM])
 
@@ -331,33 +349,38 @@ def tile_liquidmemorycell_pb_kernel(tc, x, h, h_candidate, Wd, bd, Wu, bu, out):
                 quant(q)
             if nx <= s < NT:
                 transposes(s)
-            if ok(s - 4):
-                e2v(s - 4, 0)
+            late = [i for i in range(NT) if max(i + 4, B1) == s]
+            for i in late:
+                e2v(i, 0)
             for i in (range(NH) if s == 3 else [s - 3]):
                 if ok(i) and (s == 3 or i >= NH):
                     e1v_full(i)
-            if ok(s - 4):
-                e2v(s - 4, 1)
+            for i in late:
+                e2v(i, 1)
+            if nx <= s + 1 < NT and s + 1 >= EV:
+                spread_pass0(s + 1)
             if nx <= q < NT and QW == 2 and QS <= s < QE:
                 quant(q, 0)
             if NH <= s - 2 < NT:
                 passes([s - 2], range(NG))
-            if ok(s - 3):
-                e1s(s - 3)
+            for i in range(NT):
+                if s == max(i + 3, G1):
+                    e1s(i)
             for i in range(NT):
                 first = max([f for f in ROOTS if f <= i])
                 last = min([f for f in ROOTS + (NT,) if f > i]) - 1
                 if s == last + 7 + (i - first if i < NBATCH else 0):
                     e3(i)
-            if ok(s - 4):
-                e2v(s - 4, 2)
+            for i in late:
+                e2v(i, 2)
             if nx <= q < NT and QW == 1 and QS <= s < QE:
                 quant(q)
             if nx <= q < NT and QW == 2 and QS <= s < QE:
                 quant(q, 1)
-            if ok(s - 4):
-                e2v(s - 4, 3)
-                if s - 4 + XB < NT:
-                    load_x(s - 4 + XB)
-            if ok(s - 5):
-                e2s(s - 5)
+            for i in late:
+                e2v(i, 3)
+                if i + XB < NT:
+                    load_x(i + XB)
+            for i in range(NT):
+                if max(i + 5, B1 + 1) == s:
+                    e2s(i)

@@ -43,7 +43,8 @@ QE = 15
 G1 = 3
 B1 = 5
 HCP = 7
-EV = 99
+EV = 9
+EVL = 2
 
 
 def tile_liquidmemorycell_pb_kernel(tc, x, h, h_candidate, Wd, bd, Wu, bu, out):
@@ -126,7 +127,7 @@ def tile_liquidmemorycell_pb_kernel(tc, x, h, h_candidate, Wd, bd, Wu, bu, out):
         evens = {}
 
         def spread_pass0(i):
-            evens[i] = work.tile([P, 2 * P], F32, name="even", tag="even", bufs=2)
+            evens[i] = work.tile([P, 2 * P], F32, name="even", tag="even", bufs=3)
             nc.vector.tensor_copy(out=evens[i][:].rearrange("p (u w) -> p u w", u=2),
                                   in_=xs[i][:, 0:4 * P].bitcast(F32).rearrange("p (w u) -> p u w", u=2))
 
@@ -357,8 +358,8 @@ def tile_liquidmemorycell_pb_kernel(tc, x, h, h_candidate, Wd, bd, Wu, bu, out):
                     e1v_full(i)
             for i in late:
                 e2v(i, 1)
-            if nx <= s + 1 < NT and s + 1 >= EV:
-                spread_pass0(s + 1)
+            if EV <= s + EVL < NT:
+                spread_pass0(s + EVL)
             if nx <= q < NT and QW == 2 and QS <= s < QE:
                 quant(q, 0)
             if NH <= s - 2 < NT:

@@ -27,7 +27,7 @@ BETA = B0 / (A0 * (A0 + B0))
 C2 = A0 / B0
 
 MANUAL = True
-XB = 8
+XB = 9
 NH = 4
 ORDER = "x0 x1 x2 x3 w0 w1 w2 w3 w4 w5 w6 w7"
 SHARE = (0, 1, 4)
@@ -43,8 +43,9 @@ QE = 15
 G1 = 3
 B1 = 5
 HCP = 7
-EV = 9
+EV = 10
 EVL = 2
+GTB = 3
 
 
 def tile_liquidmemorycell_pb_kernel(tc, x, h, h_candidate, Wd, bd, Wu, bu, out):
@@ -221,7 +222,7 @@ def tile_liquidmemorycell_pb_kernel(tc, x, h, h_candidate, Wd, bd, Wu, bu, out):
 
         def e1s(i, half=None):
             if half in (None, 0):
-                gts[i] = work.tile([P, NOUT], F32, name="gt", tag="gt", bufs=4)
+                gts[i] = work.tile([P, NOUT], F32, name="gt", tag="gt", bufs=GTB)
             cols = slice(0, NOUT) if half is None else slice(MEM * half, MEM * (half + 1))
             nc.scalar.activation(out=gts[i][:, cols], in_=ss[i][:, cols], func=ACT.Sigmoid, scale=-1.0)
 

from contextlib import ExitStack
import math

import concourse.mybir as mybir
from concourse.masks import make_identity

F32 = mybir.dt.float32
BF16 = mybir.dt.bfloat16
U32 = mybir.dt.uint32
U8 = mybir.dt.uint8
FP8X4 = mybir.dt.float8_e4m3fn_x4
ALU = mybir.AluOpType
ACT = mybir.ActivationFunctionType

P = 128
B, IN_DIM, MEM = 2048, 3840, 256
DIN = MEM + IN_DIM
NT = B // P
NG = DIN // 512
NOUT = 2 * MEM
FLOPS = 2 * B * DIN * NOUT

A0 = 0.1 + 1e-6
B0 = 10.0 - 0.1
LNK = math.log((A0 + B0) / A0)
BETA = B0 / (A0 * (A0 + B0))
C2 = A0 / B0

MANUAL = True
XB = 9
NH = 4
ORDER = "x0 x1 x2 x3 w0 w1 w2 w3 w4 w5 w6 w7"
SHARE = (0, 1, 4)
NBATCH = 12
ROOTS = (0, 4, 8, 12, 15)
HB = 8
NWARM = (2, 2, 2, 12)
LATE_NORM = (2, 3, 4, 5)
CB = 4
QW = 1
QS = 9
QE = 15
G1 = 3
B1 = 5
HCP = 7
EV = 10
EVL = 2
GTB = 3


def tile_liquidmemorycell_pb_kernel(tc, x, h, h_candidate, Wd, bd, Wu, bu, out):
    nc = tc.nc
    with ExitStack() as ctx:
        const = ctx.enter_context(tc.tile_pool(name="const", bufs=1))
        xpool = ctx.enter_context(tc.tile_pool(name="xpool", bufs=XB))
        work = ctx.enter_context(tc.tile_pool(name="work", bufs=2))
        psum = ctx.enter_context(tc.psum_pool(name="psum", bufs=1))
        free_banks = list(range(8))

        def take_bank(name, shape, dtype):
            b = free_banks[0]
            free_banks.remove(b)
            return b, psum.tile(shape, dtype, name=name, tag="bank%d" % b)
        if MANUAL:
            ctx.enter_context(tc.manual_schedule())

        xv = x.rearrange("(p t) k -> p t k", t=NT)
        ov = out.rearrange("(p t) f -> p t f", t=NT)
        hv = h.rearrange("(p t) f -> p t f", t=NT)

        ident = const.tile([P, P], F32, name="ident")
        make_identity(nc, ident[:])
        ones = const.tile([P, P], BF16, name="ones")
        nc.vector.memset(ones[:], 1.0)
        brow = const.tile([P, NOUT], BF16, name="brow")
        nc.vector.memset(brow[:], 0.0)
        nc.scalar.dma_start(out=brow[0:1, 0:MEM], in_=bd.unsqueeze(0))
        nc.scalar.dma_start(out=brow[0:1, MEM:NOUT], in_=bu.unsqueeze(0))
        warm = const.tile([P, 1], F32, name="warm")
        nc.vector.memset(warm[:], 0.0)
        warm2 = const.tile([P, 1], F32, name="warm2")
        nc.scalar.activation(out=warm2[:], in_=warm[:], func=ACT.Sigmoid)
        neghalf = const.tile([P, 4], F32, name="neghalf")
        nc.gpsimd.memset(neghalf[:], -0.5)
        poshalf = const.tile([P, NT], F32, name="poshalf")
        nc.gpsimd.memset(poshalf[:], 0.5)

        hc_all = const.tile([P, NT * MEM], BF16, name="hc_all")
        wr = [const.tile([P, NG, 4, MEM], BF16, name="wr%d" % mi) for mi in range(2)]
        wcodes = const.tile([P, NG * NOUT], U32, name="wcodes", align_bytes=64)
        wscl = const.tile([P, NG * NOUT], U8, name="wscl", align_bytes=64)
        bias = const.tile([P, NOUT], F32, name="bias")
        hsq = const.tile([P, NT], F32, name="hsq")
        hmx = const.tile([P, NT], F32, name="hmx")
        hn = const.tile([P, NT], F32, name="hn")
        junkh = const.tile([P, MEM], BF16, name="junkh")
        junkm = const.tile([P, MEM], BF16, name="junkm")

        xs = {}
        grp = {}
        codes = {}
        scl = {}
        acc = {}
        gts = {}
        ss = {}
        ms = {}
        rms = {}

        def load_x(i):
            xt = xpool.tile([P, DIN], BF16, name="xt", tag="xt")
            nc.sync.dma_start(out=xt[:, 0:MEM], in_=hv[:, i, :])
            cuts = [MEM, 1024, 2048, 3072, DIN] if i == 0 else [MEM, DIN]
            for lo, hi in zip(cuts[:-1], cuts[1:]):
                nc.sync.dma_start(out=xt[:, lo:hi], in_=xv[:, i, lo - MEM:hi - MEM])
            xs[i] = xt

        def load_w(g):
            for mi, w in enumerate((Wd, Wu)):
                rows = w[512 * g:512 * (g + 1), :]
                if g == 0:
                    nc.sync.dma_start(out=wr[mi][:, 0], in_=rows.rearrange("(p t) n -> p t n", t=4))
                else:
                    nc.sync.dma_start(
                        out=wr[mi][:, g].rearrange("p (u e) n -> p u e n", u=2),
                        in_=rows.rearrange("(u p e) n -> p u e n", u=2, e=2),
                    )

        evens = {}

        def spread_pass0(i):
            evens[i] = work.tile([P, 2 * P], F32, name="even", tag="even", bufs=3)
            nc.vector.tensor_copy(out=evens[i][:].rearrange("p (u w) -> p u w", u=2),
                                  in_=xs[i][:, 0:4 * P].bitcast(F32).rearrange("p (w u) -> p u w", u=2))

        def t_bank(i, b, on_vector=False):
            if b == 0:
                grp[i] = work.tile([P, DIN], BF16, name="grp", tag="grp", bufs=3, align_bytes=64)
            xw = xs[i][:].bitcast(F32)
            bno, tp = take_bank("tp", [P, 512], F32)
            for s in range(4):
                j = 4 * b + s
                if j >= 2:
                    src = xw[:, P * j:P * (j + 1)]
                elif i in evens:
                    src = evens[i][:, P * j:P * (j + 1)]
                else:
                    src = xw[:, j:2 * P:2]
                nc.tensor.transpose(tp[:, P * s:P * (s + 1)], src, ident[:])
            dst = grp[i][:].bitcast(F32)[:, 512 * b:512 * (b + 1)].rearrange(
                "p (g r u) -> p g r u", g=2, u=2)
            srcv = tp[:].rearrange("p (g u r) -> p g r u", g=2, u=2)
            if on_vector:
                nc.vector.tensor_copy(out=dst, in_=srcv)
            else:
                nc.scalar.copy(out=dst, in_=srcv)
            free_banks.append(bno)

        def quant(i, half=None):
            if half in (None, 0):
                codes[i] = work.tile([P, NG * P], U32, name="codes", tag="codes", bufs=CB, align_bytes=64)
                scl[i] = work.tile([P, NG * P], U8, name="scl", tag="scl", bufs=CB, align_bytes=64)
            w = NG * P // 2
            cols = slice(0, 2 * w) if half is None else slice(w * half, w * (half + 1))
            nc.vector.quantize_mx(out=codes[i][:, cols].bitcast(FP8X4), scales=scl[i][:, cols],
                                  in_=grp[i][:, 4 * cols.start:4 * cols.stop])

        wgs = {}

        def w_copy(g, mi, on_vector):
            if mi == 0:
                wgs[g] = work.tile([P, NOUT, 4], BF16, name="wg", tag="wg", bufs=3, align_bytes=64)
            dst = wgs[g][:, MEM * mi:MEM * (mi + 1), :].rearrange("p (c i) t -> p c t i", i=4)
            src = wr[mi][:, g].rearrange("p t (c i) -> p c t i", i=4)
            if on_vector:
                nc.vector.tensor_copy(out=dst, in_=src)
            else:
                nc.scalar.copy(out=dst, in_=src)

        def w_quant(g):
            nc.vector.quantize_mx(
                out=wcodes[:, NOUT * g:NOUT * (g + 1)].bitcast(FP8X4),
                scales=wscl[:, NOUT * g:NOUT * (g + 1)],
                in_=wgs[g][:].rearrange("p n t -> p (n t)"),
            )

        npass = {}
        accb = {}

        def mx(i, g):
            if i not in npass:
                npass[i] = 0
                accb[i], acc[i] = take_bank("acc", [P, NOUT], F32)
            npass[i] += 1
            nc.tensor.matmul_mx(
                out=acc[i][:],
                lhsT=codes[i][:, P * g:P * (g + 1)].bitcast(FP8X4),
                lhsT_scale=scl[i][:, P * g:P * (g + 1)],
                rhs=wcodes[:, NOUT * g:NOUT * (g + 1)].bitcast(FP8X4),
                rhs_scale=wscl[:, NOUT * g:NOUT * (g + 1)],
                start=(npass[i] == 1),
                stop=(npass[i] == NG),
            )

        def h_square(i):
            nc.scalar.activation(out=junkh[:], in_=xs[i][:, 0:MEM], func=ACT.Square,
                                 accum_out=hsq[:, i:i + 1])
            if i % HB == HB - 1:
                cols = slice(i - HB + 1, i + 1)
                nc.gpsimd.tensor_scalar_max(out=hmx[:, cols], in0=hsq[:, cols], scalar1=1e-12)
                nc.gpsimd.tensor_tensor(out=hn[:, cols], in0=hmx[:, cols], in1=poshalf[:, cols], op=ALU.pow)

        def e1v_full(i):
            ss[i] = work.tile([P, NOUT], F32, name="s", tag="s", bufs=5)
            nc.vector.tensor_tensor(out=ss[i][:], in0=acc[i][:], in1=bias[:], op=ALU.add)
            free_banks.append(accb[i])

        def e1v(i, half):
            if half == 0:
                ss[i] = work.tile([P, NOUT], F32, name="s", tag="s", bufs=3)
            cols = slice(MEM * half, MEM * (half + 1))
            nc.vector.tensor_tensor(out=ss[i][:, cols], in0=acc[i][:, cols], in1=bias[:, cols], op=ALU.add)

        def e1s(i, half=None):
            if half in (None, 0):
                gts[i] = work.tile([P, NOUT], F32, name="gt", tag="gt", bufs=GTB)
            cols = slice(0, NOUT) if half is None else slice(MEM * half, MEM * (half + 1))
            nc.scalar.activation(out=gts[i][:, cols], in_=ss[i][:, cols], func=ACT.Sigmoid, scale=-1.0)

        ws = {}

        def e2v(i, step):
            hs = xs[i][:, 0:MEM]
            cs = hc_all[:, MEM * i:MEM * (i + 1)]
            gt = gts[i]
            if step == 0:
                w1 = work.tile([P, MEM], F32, name="w1", tag="w1", bufs=2)
                nc.vector.scalar_tensor_tensor(out=w1[:], in0=gt[:, 0:MEM], scalar=C2, in1=hs,
                                               op0=ALU.add, op1=ALU.mult)
                ws[i] = w1
            elif step == 1:
                w2 = work.tile([P, MEM], F32, name="w2", tag="w2", bufs=2)
                nc.vector.scalar_tensor_tensor(out=w2[:], in0=ws[i][:], scalar=BETA, in1=cs,
                                               op0=ALU.mult, op1=ALU.subtract)
                ws[i] = w2
            elif step == 2:
                w3 = work.tile([P, MEM], F32, name="w3", tag="w3", bufs=2)
                nc.vector.tensor_tensor(out=w3[:], in0=ws[i][:], in1=gt[:, MEM:NOUT], op=ALU.mult)
                ws[i] = w3
            else:
                m = work.tile([P, MEM], F32, name="m", tag="m", bufs=8)
                nc.vector.tensor_tensor(out=m[:], in0=ws[i][:], in1=cs, op=ALU.add)
                ms[i] = m

        smq = {}

        def e2s(i):
            m = ms[i]
            first = max([f for f in ROOTS if f <= i])
            n = min([f for f in ROOTS + (NT,) if f > i]) - first
            b, j = (first, i - first)
            if j == 0:
                smq[b] = work.tile([P, n], F32, name="sm", tag="sm%d" % n, bufs=4)
            nc.scalar.activation(out=junkm[:], in_=m[:], func=ACT.Square, accum_out=smq[b][:, j:j + 1])
            if j == n - 1:
                sx = work.tile([P, n], F32, name="sx", tag="sx%d" % n, bufs=4)
                nc.gpsimd.tensor_scalar_max(out=sx[:], in0=smq[b][:], scalar1=1e-24)
                rm = work.tile([P, n], F32, name="rm", tag="rm%d" % n, bufs=4)
                nc.gpsimd.tensor_tensor(out=rm[:], in0=sx[:], in1=neghalf[:, 0:n], op=ALU.pow)
                for k in range(n):
                    rms[i - n + 1 + k] = rm[:, k:k + 1]

        def e3(i):
            o = work.tile([P, MEM], F32, name="o", tag="o", bufs=8)
            nc.vector.tensor_scalar(out=o[:], in0=ms[i][:], scalar1=rms[i],
                                    scalar2=hn[:, i:i + 1], op0=ALU.mult, op1=ALU.mult)
            nc.sync.dma_start(out=ov[:, i, :], in_=o[:])

        cflat = h_candidate.rearrange("(p t) f -> p (t f)", t=NT)
        cut = 4 * MEM
        order = [(o[0], int(o[1:])) for o in ORDER.split()]
        for kind, j in order:
            if kind == "x":
                load_x(j)
            else:
                load_w(j)
        nx = 1 + max([j for kind, j in order if kind == "x"])
        for i in range(nx, HCP):
            load_x(i)
        nc.sync.dma_start(out=hc_all[:, 0:cut], in_=cflat[:, 0:cut])
        for i in range(HCP, XB):
            load_x(i)
        nc.sync.dma_start(out=hc_all[:, cut:NT * MEM], in_=cflat[:, cut:NT * MEM])

        def transposes(i):
            for b in range(4):
                t_bank(i, b, on_vector=(i in SHARE and b % 2 == 1))
            if i not in LATE_NORM:
                h_square(i)

        def passes(tiles, gs):
            for g in gs:
                for i in tiles:
                    mx(i, g)

        def ok(i):
            return 0 <= i < NT

        xq = []
        wq = []
        n = len(order)
        for kslot in range(n + 2):
            if kslot < n:
                kind, j = order[kslot]
                if kind == "x":
                    transposes(j)
                    if j < NH:
                        wb, wps = take_bank("warmup", [P, NOUT], F32)
                        for r in range(NWARM[j]):
                            nc.tensor.matmul(out=wps[:], lhsT=ones[:], rhs=brow[:], start=True, stop=True)
                        free_banks.append(wb)
                else:
                    w_copy(j, 0, True)
                    w_copy(j, 1, False)
            if kslot >= 2:
                kind, j = order[kslot - 2]
                if kind == "x" and j < NH:
                    passes([j], wq)
                    xq.append(j)
                elif kind == "w":
                    passes(xq, [j])
                    wq.append(j)
            if 1 <= kslot <= n:
                kind, j = order[kslot - 1]
                if kind == "x":
                    quant(j)
                else:
                    w_quant(j)
            if kslot == 0:
                bb, bias_ps = take_bank("bias_ps", [P, NOUT], F32)
                nc.tensor.matmul(out=bias_ps[:], lhsT=ones[:], rhs=brow[:], start=True, stop=True)
                nc.vector.tensor_scalar_add(out=bias[:, 0:MEM], in0=bias_ps[:, 0:MEM], scalar1=LNK)
                nc.vector.tensor_copy(out=bias[:, MEM:NOUT], in_=bias_ps[:, MEM:NOUT])
                free_banks.append(bb)

        for i in LATE_NORM:
            h_square(i)

        for s in range(3, NT + 8):
            q = s - 1
            if nx <= q < NT and (QW == 0 or s < QS or s >= QE):
                quant(q)
            if nx <= s < NT:
                transposes(s)
            late = [i for i in range(NT) if max(i + 4, B1) == s]
            for i in late:
                e2v(i, 0)
            for i in (range(NH) if s == 3 else [s - 3]):
                if ok(i) and (s == 3 or i >= NH):
                    e1v_full(i)
            for i in late:
                e2v(i, 1)
            if EV <= s + EVL < NT:
                spread_pass0(s + EVL)
            if nx <= q < NT and QW == 2 and QS <= s < QE:
                quant(q, 0)
            if NH <= s - 2 < NT:
                passes([s - 2], range(NG))
            for i in range(NT):
                if s == max(i + 3, G1):
                    e1s(i)
            for i in range(NT):
                first = max([f for f in ROOTS if f <= i])
                last = min([f for f in ROOTS + (NT,) if f > i]) - 1
                if s == last + 7 + (i - first if i < NBATCH else 0):
                    e3(i)
            for i in late:
                e2v(i, 2)
            if nx <= q < NT and QW == 1 and QS <= s < QE:
                quant(q)
            if nx <= q < NT and QW == 2 and QS <= s < QE:
                quant(q, 1)
            for i in late:
                e2v(i, 3)
                if i + XB < NT:
                    load_x(i + XB)
            for i in range(NT):
                if max(i + 5, B1 + 1) == s:
                    e2s(i)
